import numpy as np
import ml_dtypes


def mxq(x, axis, fmt="e4m3"):
    dtype, down = {"e4m3": (ml_dtypes.float8_e4m3fn, 7), "e5m2": (ml_dtypes.float8_e5m2, 14)}[fmt]
    v = np.moveaxis(np.asarray(x, np.float32).astype(ml_dtypes.bfloat16).astype(np.float64), axis, -1)
    blocks = v.reshape(v.shape[:-1] + (-1, 32))
    amax = np.abs(blocks).max(-1, keepdims=True)
    byte = np.maximum(np.where(amax > 0, np.frexp(amax)[1] - 1 + 127, 0) - down, 1)
    scale = np.exp2(byte - 127.0)
    codes = (blocks / scale).astype(np.float32).astype(dtype).astype(np.float64)
    return np.moveaxis((codes * scale).reshape(v.shape), -1, axis)


WIDE = False


def mx_kscale(k):
    if not WIDE:
        return np.ones(k)
    levels = np.array([10, -10, 5, -5, 0])
    a = np.random.permutation(np.resize(levels, k // 512 * 4)).reshape(k // 512, 4)
    idx = np.arange(k)
    return np.exp2(a[idx // 512, idx % 128 // 32])


BF16 = ml_dtypes.bfloat16


def bf(x):
    return np.asarray(x, np.float32).astype(BF16)


def f64(x):
    return np.asarray(x).astype(np.float64)


N, D_IN, HEADS, DPH = 4096, 512, 2, 64
EDGE_P = 0.01


def setup_inputs():
    s, t = mx_kscale(D_IN), mx_kscale(N)
    edges = (np.random.random((N, N)) < EDGE_P).astype(np.float64)
    a = (edges + 0.1 * np.random.standard_normal((N, N))) / np.sqrt(EDGE_P * N)
    return {"H": bf(np.random.standard_normal((N, D_IN)) * s / t[:, None]),
            "adj": bf(a * t),
            "W": bf(np.random.standard_normal((HEADS, D_IN, DPH)) / np.sqrt(D_IN) / s[:, None]),
            "b": bf(np.random.standard_normal((HEADS, DPH)) * 0.2)}


def reference(H, adj, W, b):
    H_ = mxq(f64(H), 1, "e4m3") @ mxq(f64(W), 1, "e4m3")
    out = (mxq(f64(adj), 1, "e4m3") @ mxq(H_, 1, "e4m3")) + f64(b)[:, None, :]
    return np.transpose(out, (1, 0, 2)).reshape(H.shape[0], HEADS * DPH)

@@ -1,0 +1,200 @@
+from contextlib import ExitStack
+
+import concourse.mybir as mybir
+from concourse.masks import make_identity
+
+F32 = mybir.dt.float32
+BF16 = mybir.dt.bfloat16
+U32 = mybir.dt.uint32
+U8 = mybir.dt.uint8
+FP8X4 = mybir.dt.float8_e4m3fn_x4
+ADD = mybir.AluOpType.add
+
+P = 128
+NODES = 4096
+D_IN = 512
+D_OUT = 128
+
+FLOPS = 2 * NODES * D_IN * D_OUT + 2 * NODES * NODES * D_OUT
+
+H_UNITS = 4
+A_CHUNKS = 16
+A_BUFS = 6
+VECTOR_BANK = 3
+
+
+def tile_graphlayer_t_kernel(tc, H, adj, W, b, out):
+    nc = tc.nc
+    with ExitStack() as ctx:
+        const = ctx.enter_context(tc.tile_pool(name="const", bufs=1))
+        hpool = ctx.enter_context(tc.tile_pool(name="hpool", bufs=H_UNITS))
+        apool = ctx.enter_context(tc.tile_pool(name="apool", bufs=A_BUFS))
+        gpool = ctx.enter_context(tc.tile_pool(name="gpool", bufs=3))
+        cpool = ctx.enter_context(tc.tile_pool(name="cpool", bufs=3))
+        opool = ctx.enter_context(tc.tile_pool(name="opool", bufs=3))
+        ring = ctx.enter_context(tc.psum_pool(name="ring", bufs=6))
+        accp = ctx.enter_context(tc.psum_pool(name="accp", bufs=2))
+        ctx.enter_context(tc.manual_schedule())
+
+        h_view = H.rearrange("(g p e) d -> p g (e d)", p=P, e=2)
+        adj_view = adj.rearrange("(c p s) k -> c p (s k)", p=P, s=2)
+        out_view = out.rearrange("(c p s) n -> c p (s n)", p=P, s=2)
+
+        ident = const.tile([P, P], F32)
+        make_identity(nc, ident[:])
+        ones = const.tile([P, P], BF16)
+        nc.vector.memset(ones[:], 1.0)
+        b_row = const.tile([P, 2 * P], BF16)
+        nc.vector.memset(b_row[:], 0.0)
+        b_flat = b.rearrange("(o h) c -> o (h c)", o=1)
+        nc.scalar.dma_start(out=b_row[0:1, 0:P], in_=b_flat)
+        nc.scalar.dma_start(out=b_row[0:1, P : 2 * P], in_=b_flat)
+        bias = const.tile([P, 2 * P], F32)
+
+        w_raw = const.tile([P, 4, P], BF16)
+        nc.sync.dma_start(
+            out=w_raw[:], in_=W.rearrange("h (u p e) c -> p (h u) (e c)", u=2, p=P, e=2)
+        )
+        h_tiles = []
+        for hc in range(H_UNITS):
+            h_sb = hpool.tile([P, 4096], BF16, name="h_sb")
+            nc.sync.dma_start(
+                out=h_sb[:].rearrange("p (g x) -> p g x", g=4),
+                in_=h_view[:, 4 * hc : 4 * hc + 4, :],
+            )
+            h_tiles.append(h_sb)
+        a_tiles = {}
+        for c in range(A_BUFS):
+            a_sb = apool.tile([P, 8192], BF16, name="a_sb")
+            nc.sync.dma_start(out=a_sb[:], in_=adj_view[c])
+            a_tiles[c] = a_sb
+
+        w_grp = const.tile([P, 4 * P], BF16, align_bytes=64)
+        for h in range(2):
+            nc.vector.tensor_copy(
+                out=w_grp[:, 256 * h : 256 * h + 256].rearrange(
+                    "p (c u e) -> p c u e", u=2, e=2
+                ),
+                in_=w_raw[:, 2 * h : 2 * h + 2, :].rearrange("p u (e c) -> p c u e", e=2),
+            )
+        w_codes = const.tile([P, P], U32, align_bytes=64)
+        w_scales = const.tile([P, P], U8, align_bytes=64)
+        nc.vector.quantize_mx(out=w_codes[:].bitcast(FP8X4), scales=w_scales[:], in_=w_grp[:])
+
+        p_grp = const.tile([P, 4096], BF16, align_bytes=64)
+        p_codes = const.tile([P, 1024], U32, align_bytes=64)
+        p_scales = const.tile([P, 1024], U8, align_bytes=64)
+
+        def transpose_unit(words):
+            grouped = gpool.tile([P, 4096], BF16, align_bytes=64, name="grouped")
+            for bank in range(4):
+                tp = ring.tile([P, 512], F32, name="tp")
+                for q in range(4):
+                    blk = 4 * bank + q
+                    nc.tensor.transpose(
+                        tp[:, P * q : P * q + P], words[:, P * blk : P * blk + P], ident[:]
+                    )
+                dst = (
+                    grouped[:, 1024 * bank : 1024 * bank + 1024]
+                    .bitcast(F32)
+                    .rearrange("p (g m u) -> p g m u", g=2, u=2)
+                )
+                src = tp[:].rearrange("p (g u m) -> p g m u", g=2, u=2)
+                if bank == VECTOR_BANK:
+                    nc.vector.tensor_copy(out=dst, in_=src)
+                else:
+                    nc.scalar.copy(out=dst, in_=src)
+            return grouped
+
+        def quantise_unit(grouped):
+            codes = cpool.tile([P, 1024], U32, align_bytes=64, name="codes")
+            scales = cpool.tile([P, 1024], U8, align_bytes=64, name="scales")
+            nc.vector.quantize_mx(out=codes[:].bitcast(FP8X4), scales=scales[:], in_=grouped[:])
+            return codes, scales
+
+        def project(hc, codes, scales):
+            for gl in range(2):
+                g = 2 * hc + gl
+                pp = accp.tile([P, 512], F32, name="acc")
+                for t in range(4):
+                    cols = slice(P * (4 * gl + t), P * (4 * gl + t) + P)
+                    nc.tensor.matmul_mx(
+                        out=pp[:, P * t : P * t + P],
+                        lhsT=codes[:, cols].bitcast(FP8X4),
+                        lhsT_scale=scales[:, cols],
+                        rhs=w_codes[:].bitcast(FP8X4),
+                        rhs_scale=w_scales[:],
+                        start=True,
+                        stop=True,
+                    )
+                dst = p_grp[:, 512 * g : 512 * g + 512].rearrange("p (n t) -> p n t", t=4)
+                src = pp[:].rearrange("p (t n) -> p n t", t=4)
+                if gl == 0:
+                    nc.vector.tensor_copy(out=dst, in_=src)
+                else:
+                    nc.scalar.copy(out=dst, in_=src)
+            nc.vector.quantize_mx(
+                out=p_codes[:, 256 * hc : 256 * hc + 256].bitcast(FP8X4),
+                scales=p_scales[:, 256 * hc : 256 * hc + 256],
+                in_=p_grp[:, 1024 * hc : 1024 * hc + 1024],
+            )
+
+        def aggregate(codes, scales, acc_cols):
+            for g in range(8):
+                cols = slice(P * g, P * g + P)
+                nc.tensor.matmul_mx(
+                    out=acc_cols,
+                    lhsT=codes[:, cols].bitcast(FP8X4),
+                    lhsT_scale=scales[:, cols],
+                    rhs=p_codes[:, cols].bitcast(FP8X4),
+                    rhs_scale=p_scales[:, cols],
+                    start=(g == 0),
+                    stop=(g == 7),
+                )
+
+        def finish_pair(c, acc):
+            res = opool.tile([P, 2 * P], F32, name="res")
+            nc.vector.tensor_tensor(out=res[:], in0=acc[:, 0 : 2 * P], in1=bias[:], op=ADD)
+            nc.sync.dma_start(out=out_view[c], in_=res[:])
+
+        n_units = H_UNITS + 2 * A_CHUNKS
+        grouped_of = {}
+        quantised_of = {}
+        acc_of = {}
+        pending = []
+        for j in range(n_units + 3):
+            done = list(pending)
+            pending = []
+            if 0 <= j - 1 < n_units:
+                quantised_of[j - 1] = quantise_unit(grouped_of[j - 1])
+            if j < n_units:
+                if j < H_UNITS:
+                    words = h_tiles[j][:].bitcast(F32)
+                else:
+                    c, s = divmod(j - H_UNITS, 2)
+                    words = a_tiles[c][:, 4096 * s : 4096 * s + 4096].bitcast(F32)
+                grouped_of[j] = transpose_unit(words)
+                if j >= H_UNITS and s == 1 and c + A_BUFS < A_CHUNKS:
+                    a_sb = apool.tile([P, 8192], BF16, name="a_sb")
+                    nc.sync.dma_start(out=a_sb[:], in_=adj_view[c + A_BUFS])
+                    a_tiles[c + A_BUFS] = a_sb
+            if j == 1:
+                bias_ps = accp.tile([P, 512], F32, name="acc")
+                nc.tensor.matmul(
+                    out=bias_ps[:, 0 : 2 * P], lhsT=ones[:], rhs=b_row[:], start=True, stop=True
+                )
+                nc.vector.tensor_copy(out=bias[:], in_=bias_ps[:, 0 : 2 * P])
+            if 0 <= j - 2 < n_units:
+                codes, scales = quantised_of[j - 2]
+                if j - 2 < H_UNITS:
+                    project(j - 2, codes, scales)
+                else:
+                    c2, s2 = divmod(j - 2 - H_UNITS, 2)
+                    if s2 == 0:
+                        acc = accp.tile([P, 512], F32, name="acc")
+                        acc_of[c2] = acc
+                    aggregate(codes, scales, acc_of[c2][:, P * s2 : P * s2 + P])
+                    if s2 == 1:
+                        pending.append(c2)
+            for c3 in done:
+                finish_pair(c3, acc_of[c3])

@@ -31,7 +31,7 @@ def tile_graphlayer_t_kernel(tc, H, adj, W, b, out):
         apool = ctx.enter_context(tc.tile_pool(name="apool", bufs=A_BUFS))
         gpool = ctx.enter_context(tc.tile_pool(name="gpool", bufs=3))
         cpool = ctx.enter_context(tc.tile_pool(name="cpool", bufs=3))
-        opool = ctx.enter_context(tc.tile_pool(name="opool", bufs=3))
+        opool = ctx.enter_context(tc.tile_pool(name="opool", bufs=A_CHUNKS))
         ring = ctx.enter_context(tc.psum_pool(name="ring", bufs=6))
         accp = ctx.enter_context(tc.psum_pool(name="accp", bufs=2))
         ctx.enter_context(tc.manual_schedule())

@@ -30,15 +30,14 @@ def tile_graphlayer_t_kernel(tc, H, adj, W, b, out):
         hpool = ctx.enter_context(tc.tile_pool(name="hpool", bufs=H_UNITS))
         apool = ctx.enter_context(tc.tile_pool(name="apool", bufs=A_BUFS))
         gpool = ctx.enter_context(tc.tile_pool(name="gpool", bufs=3))
-        cpool = ctx.enter_context(tc.tile_pool(name="cpool", bufs=3))
-        opool = ctx.enter_context(tc.tile_pool(name="opool", bufs=A_CHUNKS))
-        ring = ctx.enter_context(tc.psum_pool(name="ring", bufs=6))
-        accp = ctx.enter_context(tc.psum_pool(name="accp", bufs=2))
+        cpool = ctx.enter_context(tc.tile_pool(name="cpool", bufs=4))
+        ring = ctx.enter_context(tc.psum_pool(name="ring", bufs=7))
+        accp = ctx.enter_context(tc.psum_pool(name="accp", bufs=1))
         ctx.enter_context(tc.manual_schedule())
 
         h_view = H.rearrange("(g p e) d -> p g (e d)", p=P, e=2)
-        adj_view = adj.rearrange("(c p s) k -> c p (s k)", p=P, s=2)
-        out_view = out.rearrange("(c p s) n -> c p (s n)", p=P, s=2)
+        adj_view = adj.rearrange("(c p s) k -> c p (s k)", p=P, s=8)
+        out_view = out.rearrange("(c p s) n -> c p (s n)", p=P, s=8)
 
         ident = const.tile([P, P], F32)
         make_identity(nc, ident[:])
@@ -50,6 +49,13 @@ def tile_graphlayer_t_kernel(tc, H, adj, W, b, out):
         nc.scalar.dma_start(out=b_row[0:1, 0:P], in_=b_flat)
         nc.scalar.dma_start(out=b_row[0:1, P : 2 * P], in_=b_flat)
         bias = const.tile([P, 2 * P], F32)
+
+        def load_chunk(c):
+            a_sb = apool.tile([P, 8192], BF16, name="a_sb")
+            nc.sync.dma_start(
+                out=a_sb[:], in_=adj_view[c // 4][:, 8192 * (c % 4) : 8192 * (c % 4) + 8192]
+            )
+            return a_sb
 
         w_raw = const.tile([P, 4, P], BF16)
         nc.sync.dma_start(
@@ -65,9 +71,7 @@ def tile_graphlayer_t_kernel(tc, H, adj, W, b, out):
             h_tiles.append(h_sb)
         a_tiles = {}
         for c in range(A_BUFS):
-            a_sb = apool.tile([P, 8192], BF16, name="a_sb")
-            nc.sync.dma_start(out=a_sb[:], in_=adj_view[c])
-            a_tiles[c] = a_sb
+            a_tiles[c] = load_chunk(c)
 
         w_grp = const.tile([P, 4 * P], BF16, align_bytes=64)
         for h in range(2):
@@ -84,6 +88,13 @@ def tile_graphlayer_t_kernel(tc, H, adj, W, b, out):
         p_grp = const.tile([P, 4096], BF16, align_bytes=64)
         p_codes = const.tile([P, 1024], U32, align_bytes=64)
         p_scales = const.tile([P, 1024], U8, align_bytes=64)
+
+        res_first = [0, 4, 8, 12, 15, 16]
+        res_tiles = []
+        for i in range(5):
+            res_tiles.append(
+                const.tile([P, 256 * (res_first[i + 1] - res_first[i])], F32, name="res%d" % i)
+            )
 
         def transpose_unit(words):
             grouped = gpool.tile([P, 4096], BF16, align_bytes=64, name="grouped")
@@ -115,7 +126,7 @@ def tile_graphlayer_t_kernel(tc, H, adj, W, b, out):
         def project(hc, codes, scales):
             for gl in range(2):
                 g = 2 * hc + gl
-                pp = accp.tile([P, 512], F32, name="acc")
+                pp = ring.tile([P, 512], F32, name="tp")
                 for t in range(4):
                     cols = slice(P * (4 * gl + t), P * (4 * gl + t) + P)
                     nc.tensor.matmul_mx(
@@ -152,49 +163,71 @@ def tile_graphlayer_t_kernel(tc, H, adj, W, b, out):
                     stop=(g == 7),
                 )
 
-        def finish_pair(c, acc):
-            res = opool.tile([P, 2 * P], F32, name="res")
-            nc.vector.tensor_tensor(out=res[:], in0=acc[:, 0 : 2 * P], in1=bias[:], op=ADD)
-            nc.sync.dma_start(out=out_view[c], in_=res[:])
+        state = {"loaded": A_BUFS, "added": 0, "stored": 0}
+
+        def store_ready():
+            if state["loaded"] < A_CHUNKS:
+                return
+            while state["stored"] < 5 and res_first[state["stored"] + 1] <= state["added"]:
+                i = state["stored"]
+                c0, c1 = res_first[i], res_first[i + 1]
+                nc.sync.dma_start(
+                    out=out_view[c0 // 4][:, 256 * (c0 % 4) : 256 * (c0 % 4) + 256 * (c1 - c0)],
+                    in_=res_tiles[i][:],
+                )
+                state["stored"] = i + 1
+
+        def add_bias(c, acc):
+            i = max([k for k in range(5) if res_first[k] <= c])
+            col = 256 * (c - res_first[i])
+            nc.vector.tensor_tensor(
+                out=res_tiles[i][:, col : col + 256], in0=acc[:, 0:256], in1=bias[:], op=ADD
+            )
+            state["added"] = c + 1
+            store_ready()
 
         n_units = H_UNITS + 2 * A_CHUNKS
         grouped_of = {}
         quantised_of = {}
-        acc_of = {}
         pending = []
-        for j in range(n_units + 3):
-            done = list(pending)
+
+        def words_of(j):
+            if j < H_UNITS:
+                return h_tiles[j][:].bitcast(F32)
+            c, s = divmod(j - H_UNITS, 2)
+            return a_tiles[c][:, 4096 * s : 4096 * s + 4096].bitcast(F32)
+
+        for r in range(n_units // 2 + 1):
+            u0, u1 = 2 * r, 2 * r + 1
+            if u0 >= 1:
+                quantised_of[u0 - 1] = quantise_unit(grouped_of[u0 - 1])
+            for c, acc in pending:
+                add_bias(c, acc)
             pending = []
-            if 0 <= j - 1 < n_units:
-                quantised_of[j - 1] = quantise_unit(grouped_of[j - 1])
-            if j < n_units:
-                if j < H_UNITS:
-                    words = h_tiles[j][:].bitcast(F32)
-                else:
-                    c, s = divmod(j - H_UNITS, 2)
-                    words = a_tiles[c][:, 4096 * s : 4096 * s + 4096].bitcast(F32)
-                grouped_of[j] = transpose_unit(words)
-                if j >= H_UNITS and s == 1 and c + A_BUFS < A_CHUNKS:
-                    a_sb = apool.tile([P, 8192], BF16, name="a_sb")
-                    nc.sync.dma_start(out=a_sb[:], in_=adj_view[c + A_BUFS])
-                    a_tiles[c + A_BUFS] = a_sb
-            if j == 1:
+            if u0 < n_units:
+                grouped_of[u0] = transpose_unit(words_of(u0))
+                quantised_of[u0] = quantise_unit(grouped_of[u0])
+                grouped_of[u1] = transpose_unit(words_of(u1))
+                c = (u0 - H_UNITS) // 2
+                if c >= 0 and state["loaded"] < A_CHUNKS:
+                    a_tiles[state["loaded"]] = load_chunk(state["loaded"])
+                    state["loaded"] += 1
+                    store_ready()
+            if r == 0:
                 bias_ps = accp.tile([P, 512], F32, name="acc")
                 nc.tensor.matmul(
                     out=bias_ps[:, 0 : 2 * P], lhsT=ones[:], rhs=b_row[:], start=True, stop=True
                 )
                 nc.vector.tensor_copy(out=bias[:], in_=bias_ps[:, 0 : 2 * P])
-            if 0 <= j - 2 < n_units:
-                codes, scales = quantised_of[j - 2]
-                if j - 2 < H_UNITS:
-                    project(j - 2, codes, scales)
+            if r >= 1:
+                v0, v1 = u0 - 2, u0 - 1
+                if v0 < H_UNITS:
+                    project(v0, quantised_of[v0][0], quantised_of[v0][1])
+                    project(v1, quantised_of[v1][0], quantised_of[v1][1])
                 else:
-                    c2, s2 = divmod(j - 2 - H_UNITS, 2)
-                    if s2 == 0:
-                        acc = accp.tile([P, 512], F32, name="acc")
-                        acc_of[c2] = acc
-                    aggregate(codes, scales, acc_of[c2][:, P * s2 : P * s2 + P])
-                    if s2 == 1:
-                        pending.append(c2)
-            for c3 in done:
-                finish_pair(c3, acc_of[c3])
+                    acc = accp.tile([P, 512], F32, name="acc")
+                    aggregate(quantised_of[v0][0], quantised_of[v0][1], acc[:, 0:P])
+                    aggregate(quantised_of[v1][0], quantised_of[v1][1], acc[:, P : 2 * P])
+                    pending.append(((v0 - H_UNITS) // 2, acc))
+        for c, acc in pending:
+            add_bias(c, acc)

@@ -18,7 +18,8 @@ D_OUT = 128
 FLOPS = 2 * NODES * D_IN * D_OUT + 2 * NODES * NODES * D_OUT
 
 H_UNITS = 4
-A_CHUNKS = 16
+A_UNITS = 32
+LOAD_UNITS = 2
 A_BUFS = 6
 VECTOR_BANK = 3
 
@@ -30,9 +31,9 @@ def tile_graphlayer_t_kernel(tc, H, adj, W, b, out):
         hpool = ctx.enter_context(tc.tile_pool(name="hpool", bufs=H_UNITS))
         apool = ctx.enter_context(tc.tile_pool(name="apool", bufs=A_BUFS))
         gpool = ctx.enter_context(tc.tile_pool(name="gpool", bufs=3))
-        cpool = ctx.enter_context(tc.tile_pool(name="cpool", bufs=4))
-        ring = ctx.enter_context(tc.psum_pool(name="ring", bufs=7))
-        accp = ctx.enter_context(tc.psum_pool(name="accp", bufs=1))
+        cpool = ctx.enter_context(tc.tile_pool(name="cpool", bufs=3))
+        ring = ctx.enter_context(tc.psum_pool(name="ring", bufs=6))
+        accp = ctx.enter_context(tc.psum_pool(name="accp", bufs=2))
         ctx.enter_context(tc.manual_schedule())
 
         h_view = H.rearrange("(g p e) d -> p g (e d)", p=P, e=2)
@@ -50,11 +51,14 @@ def tile_graphlayer_t_kernel(tc, H, adj, W, b, out):
         nc.scalar.dma_start(out=b_row[0:1, P : 2 * P], in_=b_flat)
         bias = const.tile([P, 2 * P], F32)
 
-        def load_chunk(c):
-            a_sb = apool.tile([P, 8192], BF16, name="a_sb")
-            nc.sync.dma_start(
-                out=a_sb[:], in_=adj_view[c // 4][:, 8192 * (c % 4) : 8192 * (c % 4) + 8192]
-            )
+        n_loads = A_UNITS // LOAD_UNITS
+        load_cols = 4096 * LOAD_UNITS
+
+        def load_adj(i):
+            a_sb = apool.tile([P, load_cols], BF16, name="a_sb")
+            a0 = i * LOAD_UNITS
+            col = 4096 * (a0 % 8)
+            nc.sync.dma_start(out=a_sb[:], in_=adj_view[a0 // 8][:, col : col + load_cols])
             return a_sb
 
         w_raw = const.tile([P, 4, P], BF16)
@@ -70,8 +74,8 @@ def tile_graphlayer_t_kernel(tc, H, adj, W, b, out):
             )
             h_tiles.append(h_sb)
         a_tiles = {}
-        for c in range(A_BUFS):
-            a_tiles[c] = load_chunk(c)
+        for i in range(A_BUFS):
+            a_tiles[i] = load_adj(i)
 
         w_grp = const.tile([P, 4 * P], BF16, align_bytes=64)
         for h in range(2):
@@ -126,7 +130,7 @@ def tile_graphlayer_t_kernel(tc, H, adj, W, b, out):
         def project(hc, codes, scales):
             for gl in range(2):
                 g = 2 * hc + gl
-                pp = ring.tile([P, 512], F32, name="tp")
+                pp = accp.tile([P, 512], F32, name="acc")
                 for t in range(4):
                     cols = slice(P * (4 * gl + t), P * (4 * gl + t) + P)
                     nc.tensor.matmul_mx(
@@ -166,7 +170,7 @@ def tile_graphlayer_t_kernel(tc, H, adj, W, b, out):
         state = {"loaded": A_BUFS, "added": 0, "stored": 0}
 
         def store_ready():
-            if state["loaded"] < A_CHUNKS:
+            if state["loaded"] < n_loads:
                 return
             while state["stored"] < 5 and res_first[state["stored"] + 1] <= state["added"]:
                 i = state["stored"]
@@ -186,48 +190,46 @@ def tile_graphlayer_t_kernel(tc, H, adj, W, b, out):
             state["added"] = c + 1
             store_ready()
 
-        n_units = H_UNITS + 2 * A_CHUNKS
-        grouped_of = {}
-        quantised_of = {}
-        pending = []
-
         def words_of(j):
             if j < H_UNITS:
                 return h_tiles[j][:].bitcast(F32)
-            c, s = divmod(j - H_UNITS, 2)
-            return a_tiles[c][:, 4096 * s : 4096 * s + 4096].bitcast(F32)
+            i, s = divmod(j - H_UNITS, LOAD_UNITS)
+            return a_tiles[i][:, 4096 * s : 4096 * s + 4096].bitcast(F32)
 
-        for r in range(n_units // 2 + 1):
-            u0, u1 = 2 * r, 2 * r + 1
-            if u0 >= 1:
-                quantised_of[u0 - 1] = quantise_unit(grouped_of[u0 - 1])
-            for c, acc in pending:
-                add_bias(c, acc)
+        n_units = H_UNITS + A_UNITS
+        grouped_of = {}
+        quantised_of = {}
+        acc_of = {}
+        pending = []
+        for j in range(n_units + 3):
+            finished = list(pending)
             pending = []
-            if u0 < n_units:
-                grouped_of[u0] = transpose_unit(words_of(u0))
-                quantised_of[u0] = quantise_unit(grouped_of[u0])
-                grouped_of[u1] = transpose_unit(words_of(u1))
-                c = (u0 - H_UNITS) // 2
-                if c >= 0 and state["loaded"] < A_CHUNKS:
-                    a_tiles[state["loaded"]] = load_chunk(state["loaded"])
+            if 0 <= j - 1 < n_units:
+                quantised_of[j - 1] = quantise_unit(grouped_of[j - 1])
+            if j < n_units:
+                grouped_of[j] = transpose_unit(words_of(j))
+                a = j - H_UNITS
+                if a >= 0 and a % LOAD_UNITS == LOAD_UNITS - 1 and state["loaded"] < n_loads:
+                    a_tiles[state["loaded"]] = load_adj(state["loaded"])
                     state["loaded"] += 1
                     store_ready()
-            if r == 0:
+            if j == 1:
                 bias_ps = accp.tile([P, 512], F32, name="acc")
                 nc.tensor.matmul(
                     out=bias_ps[:, 0 : 2 * P], lhsT=ones[:], rhs=b_row[:], start=True, stop=True
                 )
                 nc.vector.tensor_copy(out=bias[:], in_=bias_ps[:, 0 : 2 * P])
-            if r >= 1:
-                v0, v1 = u0 - 2, u0 - 1
-                if v0 < H_UNITS:
-                    project(v0, quantised_of[v0][0], quantised_of[v0][1])
-                    project(v1, quantised_of[v1][0], quantised_of[v1][1])
+            if 0 <= j - 2 < n_units:
+                codes, scales = quantised_of[j - 2]
+                if j - 2 < H_UNITS:
+                    project(j - 2, codes, scales)
                 else:
-                    acc = accp.tile([P, 512], F32, name="acc")
-                    aggregate(quantised_of[v0][0], quantised_of[v0][1], acc[:, 0:P])
-                    aggregate(quantised_of[v1][0], quantised_of[v1][1], acc[:, P : 2 * P])
-                    pending.append(((v0 - H_UNITS) // 2, acc))
-        for c, acc in pending:
-            add_bias(c, acc)
+                    c2, s2 = divmod(j - 2 - H_UNITS, 2)
+                    if s2 == 0:
+                        acc = accp.tile([P, 512], F32, name="acc")
+                        acc_of[c2] = acc
+                    aggregate(codes, scales, acc_of[c2][:, P * s2 : P * s2 + P])
+                    if s2 == 1:
+                        pending.append(c2)
+            for c3 in finished:
+                add_bias(c3, acc_of[c3])

@@ -19,9 +19,8 @@ FLOPS = 2 * NODES * D_IN * D_OUT + 2 * NODES * NODES * D_OUT
 
 H_UNITS = 4
 A_UNITS = 32
-LOAD_UNITS = 2
-A_BUFS = 6
-VECTOR_BANK = 3
+LOAD_UNITS = 1
+A_BUFS = 12
 
 
 def tile_graphlayer_t_kernel(tc, H, adj, W, b, out):
@@ -68,10 +67,13 @@ def tile_graphlayer_t_kernel(tc, H, adj, W, b, out):
         h_tiles = []
         for hc in range(H_UNITS):
             h_sb = hpool.tile([P, 4096], BF16, name="h_sb")
-            nc.sync.dma_start(
-                out=h_sb[:].rearrange("p (g x) -> p g x", g=4),
-                in_=h_view[:, 4 * hc : 4 * hc + 4, :],
-            )
+            for half in range(2):
+                nc.sync.dma_start(
+                    out=h_sb[:, 2048 * half : 2048 * half + 2048].rearrange(
+                        "p (g x) -> p g x", g=2
+                    ),
+                    in_=h_view[:, 4 * hc + 2 * half : 4 * hc + 2 * half + 2, :],
+                )
             h_tiles.append(h_sb)
         a_tiles = {}
         for i in range(A_BUFS):
@@ -100,7 +102,7 @@ def tile_graphlayer_t_kernel(tc, H, adj, W, b, out):
                 const.tile([P, 256 * (res_first[i + 1] - res_first[i])], F32, name="res%d" % i)
             )
 
-        def transpose_unit(words):
+        def transpose_unit(words, vector_bank):
             grouped = gpool.tile([P, 4096], BF16, align_bytes=64, name="grouped")
             for bank in range(4):
                 tp = ring.tile([P, 512], F32, name="tp")
@@ -115,16 +117,22 @@ def tile_graphlayer_t_kernel(tc, H, adj, W, b, out):
                     .rearrange("p (g m u) -> p g m u", g=2, u=2)
                 )
                 src = tp[:].rearrange("p (g u m) -> p g m u", g=2, u=2)
-                if bank == VECTOR_BANK:
+                if bank == vector_bank:
                     nc.vector.tensor_copy(out=dst, in_=src)
                 else:
                     nc.scalar.copy(out=dst, in_=src)
             return grouped
 
-        def quantise_unit(grouped):
+        def quantise_unit(grouped, calls):
             codes = cpool.tile([P, 1024], U32, align_bytes=64, name="codes")
             scales = cpool.tile([P, 1024], U8, align_bytes=64, name="scales")
-            nc.vector.quantize_mx(out=codes[:].bitcast(FP8X4), scales=scales[:], in_=grouped[:])
+            w = 1024 // calls
+            for i in range(calls):
+                nc.vector.quantize_mx(
+                    out=codes[:, w * i : w * i + w].bitcast(FP8X4),
+                    scales=scales[:, w * i : w * i + w],
+                    in_=grouped[:, 4 * w * i : 4 * w * i + 4 * w],
+                )
             return codes, scales
 
         def project(hc, codes, scales):
@@ -205,9 +213,11 @@ def tile_graphlayer_t_kernel(tc, H, adj, W, b, out):
             finished = list(pending)
             pending = []
             if 0 <= j - 1 < n_units:
-                quantised_of[j - 1] = quantise_unit(grouped_of[j - 1])
+                quantised_of[j - 1] = quantise_unit(grouped_of[j - 1], 2 if j == n_units else 1)
+            for c3 in finished:
+                add_bias(c3, acc_of[c3])
             if j < n_units:
-                grouped_of[j] = transpose_unit(words_of(j))
+                grouped_of[j] = transpose_unit(words_of(j), 1 if j == n_units - 1 else 3)
                 a = j - H_UNITS
                 if a >= 0 and a % LOAD_UNITS == LOAD_UNITS - 1 and state["loaded"] < n_loads:
                     a_tiles[state["loaded"]] = load_adj(state["loaded"])
@@ -231,5 +241,3 @@ def tile_graphlayer_t_kernel(tc, H, adj, W, b, out):
                     aggregate(codes, scales, acc_of[c2][:, P * s2 : P * s2 + P])
                     if s2 == 1:
                         pending.append(c2)
-            for c3 in finished:
-                add_bias(c3, acc_of[c3])

@@ -102,9 +102,8 @@ def tile_graphlayer_t_kernel(tc, H, adj, W, b, out):
                 const.tile([P, 256 * (res_first[i + 1] - res_first[i])], F32, name="res%d" % i)
             )
 
-        def transpose_unit(words, vector_bank):
-            grouped = gpool.tile([P, 4096], BF16, align_bytes=64, name="grouped")
-            for bank in range(4):
+        def transpose_banks(words, grouped, banks):
+            for bank in banks:
                 tp = ring.tile([P, 512], F32, name="tp")
                 for q in range(4):
                     blk = 4 * bank + q
@@ -117,11 +116,10 @@ def tile_graphlayer_t_kernel(tc, H, adj, W, b, out):
                     .rearrange("p (g m u) -> p g m u", g=2, u=2)
                 )
                 src = tp[:].rearrange("p (g u m) -> p g m u", g=2, u=2)
-                if bank == vector_bank:
+                if bank == 0:
                     nc.vector.tensor_copy(out=dst, in_=src)
                 else:
                     nc.scalar.copy(out=dst, in_=src)
-            return grouped
 
         def quantise_unit(grouped, calls):
             codes = cpool.tile([P, 1024], U32, align_bytes=64, name="codes")
@@ -156,6 +154,8 @@ def tile_graphlayer_t_kernel(tc, H, adj, W, b, out):
                     nc.vector.tensor_copy(out=dst, in_=src)
                 else:
                     nc.scalar.copy(out=dst, in_=src)
+
+        def quantise_p(hc):
             nc.vector.quantize_mx(
                 out=p_codes[:, 256 * hc : 256 * hc + 256].bitcast(FP8X4),
                 scales=p_scales[:, 256 * hc : 256 * hc + 256],
@@ -212,12 +212,18 @@ def tile_graphlayer_t_kernel(tc, H, adj, W, b, out):
         for j in range(n_units + 3):
             finished = list(pending)
             pending = []
+            if j < n_units:
+                grouped = gpool.tile([P, 4096], BF16, align_bytes=64, name="grouped")
+                grouped_of[j] = grouped
+                transpose_banks(words_of(j), grouped, [0])
+            if 0 <= j - 3 < H_UNITS:
+                quantise_p(j - 3)
             if 0 <= j - 1 < n_units:
                 quantised_of[j - 1] = quantise_unit(grouped_of[j - 1], 2 if j == n_units else 1)
             for c3 in finished:
                 add_bias(c3, acc_of[c3])
             if j < n_units:
-                grouped_of[j] = transpose_unit(words_of(j), 1 if j == n_units - 1 else 3)
+                transpose_banks(words_of(j), grouped_of[j], [1, 2, 3])
                 a = j - H_UNITS
                 if a >= 0 and a % LOAD_UNITS == LOAD_UNITS - 1 and state["loaded"] < n_loads:
                     a_tiles[state["loaded"]] = load_adj(state["loaded"])

from contextlib import ExitStack

import concourse.mybir as mybir
from concourse.masks import make_identity

F32 = mybir.dt.float32
BF16 = mybir.dt.bfloat16
U32 = mybir.dt.uint32
U8 = mybir.dt.uint8
FP8X4 = mybir.dt.float8_e4m3fn_x4
ADD = mybir.AluOpType.add

P = 128
NODES = 4096
D_IN = 512
D_OUT = 128

FLOPS = 2 * NODES * D_IN * D_OUT + 2 * NODES * NODES * D_OUT

H_UNITS = 4
A_UNITS = 32
LOAD_UNITS = 1
A_BUFS = 12


def tile_graphlayer_t_kernel(tc, H, adj, W, b, out):
    nc = tc.nc
    with ExitStack() as ctx:
        const = ctx.enter_context(tc.tile_pool(name="const", bufs=1))
        hpool = ctx.enter_context(tc.tile_pool(name="hpool", bufs=H_UNITS))
        apool = ctx.enter_context(tc.tile_pool(name="apool", bufs=A_BUFS))
        gpool = ctx.enter_context(tc.tile_pool(name="gpool", bufs=3))
        cpool = ctx.enter_context(tc.tile_pool(name="cpool", bufs=3))
        ring = ctx.enter_context(tc.psum_pool(name="ring", bufs=6))
        accp = ctx.enter_context(tc.psum_pool(name="accp", bufs=2))
        ctx.enter_context(tc.manual_schedule())

        h_view = H.rearrange("(g p e) d -> p g (e d)", p=P, e=2)
        adj_view = adj.rearrange("(c p s) k -> c p (s k)", p=P, s=8)
        out_view = out.rearrange("(c p s) n -> c p (s n)", p=P, s=8)

        ident = const.tile([P, P], F32)
        make_identity(nc, ident[:])
        ones = const.tile([P, P], BF16)
        nc.vector.memset(ones[:], 1.0)
        b_row = const.tile([P, 2 * P], BF16)
        nc.vector.memset(b_row[:], 0.0)
        b_flat = b.rearrange("(o h) c -> o (h c)", o=1)
        nc.scalar.dma_start(out=b_row[0:1, 0:P], in_=b_flat)
        nc.scalar.dma_start(out=b_row[0:1, P : 2 * P], in_=b_flat)
        bias = const.tile([P, 2 * P], F32)

        n_loads = A_UNITS // LOAD_UNITS
        load_cols = 4096 * LOAD_UNITS

        def load_adj(i):
            a_sb = apool.tile([P, load_cols], BF16, name="a_sb")
            a0 = i * LOAD_UNITS
            col = 4096 * (a0 % 8)
            nc.sync.dma_start(out=a_sb[:], in_=adj_view[a0 // 8][:, col : col + load_cols])
            return a_sb

        w_raw = const.tile([P, 4, P], BF16)
        nc.sync.dma_start(
            out=w_raw[:], in_=W.rearrange("h (u p e) c -> p (h u) (e c)", u=2, p=P, e=2)
        )
        h_tiles = []
        for hc in range(H_UNITS):
            h_sb = hpool.tile([P, 4096], BF16, name="h_sb")
            for half in range(2):
                nc.sync.dma_start(
                    out=h_sb[:, 2048 * half : 2048 * half + 2048].rearrange(
                        "p (g x) -> p g x", g=2
                    ),
                    in_=h_view[:, 4 * hc + 2 * half : 4 * hc + 2 * half + 2, :],
                )
            h_tiles.append(h_sb)
        a_tiles = {}
        for i in range(A_BUFS):
            a_tiles[i] = load_adj(i)

        w_grp = const.tile([P, 4 * P], BF16, align_bytes=64)
        for h in range(2):
            nc.vector.tensor_copy(
                out=w_grp[:, 256 * h : 256 * h + 256].rearrange(
                    "p (c u e) -> p c u e", u=2, e=2
                ),
                in_=w_raw[:, 2 * h : 2 * h + 2, :].rearrange("p u (e c) -> p c u e", e=2),
            )
        w_codes = const.tile([P, P], U32, align_bytes=64)
        w_scales = const.tile([P, P], U8, align_bytes=64)
        nc.vector.quantize_mx(out=w_codes[:].bitcast(FP8X4), scales=w_scales[:], in_=w_grp[:])

        p_grp = const.tile([P, 4096], BF16, align_bytes=64)
        p_codes = const.tile([P, 1024], U32, align_bytes=64)
        p_scales = const.tile([P, 1024], U8, align_bytes=64)

        res_first = [0, 4, 8, 12, 15, 16]
        res_tiles = []
        for i in range(5):
            res_tiles.append(
                const.tile([P, 256 * (res_first[i + 1] - res_first[i])], F32, name="res%d" % i)
            )

        def transpose_banks(words, grouped, banks):
            for bank in banks:
                tp = ring.tile([P, 512], F32, name="tp")
                for q in range(4):
                    blk = 4 * bank + q
                    nc.tensor.transpose(
                        tp[:, P * q : P * q + P], words[:, P * blk : P * blk + P], ident[:]
                    )
                dst = (
                    grouped[:, 1024 * bank : 1024 * bank + 1024]
                    .bitcast(F32)
                    .rearrange("p (g m u) -> p g m u", g=2, u=2)
                )
                src = tp[:].rearrange("p (g u m) -> p g m u", g=2, u=2)
                if bank == 0:
                    nc.vector.tensor_copy(out=dst, in_=src)
                else:
                    nc.scalar.copy(out=dst, in_=src)

        def quantise_unit(grouped, calls):
            codes = cpool.tile([P, 1024], U32, align_bytes=64, name="codes")
            scales = cpool.tile([P, 1024], U8, align_bytes=64, name="scales")
            w = 1024 // calls
            for i in range(calls):
                nc.vector.quantize_mx(
                    out=codes[:, w * i : w * i + w].bitcast(FP8X4),
                    scales=scales[:, w * i : w * i + w],
                    in_=grouped[:, 4 * w * i : 4 * w * i + 4 * w],
                )
            return codes, scales

        def project(hc, codes, scales):
            for gl in range(2):
                g = 2 * hc + gl
                pp = accp.tile([P, 512], F32, name="acc")
                for t in range(4):
                    cols = slice(P * (4 * gl + t), P * (4 * gl + t) + P)
                    nc.tensor.matmul_mx(
                        out=pp[:, P * t : P * t + P],
                        lhsT=codes[:, cols].bitcast(FP8X4),
                        lhsT_scale=scales[:, cols],
                        rhs=w_codes[:].bitcast(FP8X4),
                        rhs_scale=w_scales[:],
                        start=True,
                        stop=True,
                    )
                dst = p_grp[:, 512 * g : 512 * g + 512].rearrange("p (n t) -> p n t", t=4)
                src = pp[:].rearrange("p (t n) -> p n t", t=4)
                if gl == 0:
                    nc.vector.tensor_copy(out=dst, in_=src)
                else:
                    nc.scalar.copy(out=dst, in_=src)

        def quantise_p(hc):
            nc.vector.quantize_mx(
                out=p_codes[:, 256 * hc : 256 * hc + 256].bitcast(FP8X4),
                scales=p_scales[:, 256 * hc : 256 * hc + 256],
                in_=p_grp[:, 1024 * hc : 1024 * hc + 1024],
            )

        def aggregate(codes, scales, acc_cols):
            for g in range(8):
                cols = slice(P * g, P * g + P)
                nc.tensor.matmul_mx(
                    out=acc_cols,
                    lhsT=codes[:, cols].bitcast(FP8X4),
                    lhsT_scale=scales[:, cols],
                    rhs=p_codes[:, cols].bitcast(FP8X4),
                    rhs_scale=p_scales[:, cols],
                    start=(g == 0),
                    stop=(g == 7),
                )

        state = {"loaded": A_BUFS, "added": 0, "stored": 0}

        def store_ready():
            if state["loaded"] < n_loads:
                return
            while state["stored"] < 5 and res_first[state["stored"] + 1] <= state["added"]:
                i = state["stored"]
                c0, c1 = res_first[i], res_first[i + 1]
                nc.sync.dma_start(
                    out=out_view[c0 // 4][:, 256 * (c0 % 4) : 256 * (c0 % 4) + 256 * (c1 - c0)],
                    in_=res_tiles[i][:],
                )
                state["stored"] = i + 1

        def add_bias(c, acc):
            i = max([k for k in range(5) if res_first[k] <= c])
            col = 256 * (c - res_first[i])
            nc.vector.tensor_tensor(
                out=res_tiles[i][:, col : col + 256], in0=acc[:, 0:256], in1=bias[:], op=ADD
            )
            state["added"] = c + 1
            store_ready()

        def words_of(j):
            if j < H_UNITS:
                return h_tiles[j][:].bitcast(F32)
            i, s = divmod(j - H_UNITS, LOAD_UNITS)
            return a_tiles[i][:, 4096 * s : 4096 * s + 4096].bitcast(F32)

        n_units = H_UNITS + A_UNITS
        grouped_of = {}
        quantised_of = {}
        acc_of = {}
        pending = []
        for j in range(n_units + 3):
            finished = list(pending)
            pending = []
            if j < n_units:
                grouped = gpool.tile([P, 4096], BF16, align_bytes=64, name="grouped")
                grouped_of[j] = grouped
                transpose_banks(words_of(j), grouped, [0])
            if 0 <= j - 3 < H_UNITS:
                quantise_p(j - 3)
            if 0 <= j - 1 < n_units:
                quantised_of[j - 1] = quantise_unit(grouped_of[j - 1], 2 if j == n_units else 1)
            for c3 in finished:
                add_bias(c3, acc_of[c3])
            if j < n_units:
                transpose_banks(words_of(j), grouped_of[j], [1, 2, 3])
                a = j - H_UNITS
                if a >= 0 and a % LOAD_UNITS == LOAD_UNITS - 1 and state["loaded"] < n_loads:
                    a_tiles[state["loaded"]] = load_adj(state["loaded"])
                    state["loaded"] += 1
                    store_ready()
            if j == 1:
                bias_ps = accp.tile([P, 512], F32, name="acc")
                nc.tensor.matmul(
                    out=bias_ps[:, 0 : 2 * P], lhsT=ones[:], rhs=b_row[:], start=True, stop=True
                )
                nc.vector.tensor_copy(out=bias[:], in_=bias_ps[:, 0 : 2 * P])
            if 0 <= j - 2 < n_units:
                codes, scales = quantised_of[j - 2]
                if j - 2 < H_UNITS:
                    project(j - 2, codes, scales)
                else:
                    c2, s2 = divmod(j - 2 - H_UNITS, 2)
                    if s2 == 0:
                        acc = accp.tile([P, 512], F32, name="acc")
                        acc_of[c2] = acc
                    aggregate(codes, scales, acc_of[c2][:, P * s2 : P * s2 + P])
                    if s2 == 1:
                        pending.append(c2)
